import numpy as np
import ml_dtypes


BF16 = ml_dtypes.bfloat16


def bf(x):
    return np.asarray(x, np.float32).astype(BF16)


def f64(x):
    return np.asarray(x).astype(np.float64)


E2M1 = np.array([0.0, 0.5, 1.0, 1.5, 2.0, 3.0, 4.0, 6.0, -0.0, -0.5, -1.0, -1.5, -2.0, -3.0, -4.0, -6.0])


def pack_weight(w, fmt):
    k, n = w.shape
    w = f64(bf(w)).reshape(k // 32, 32, n)
    amax = np.abs(w).max(1)
    if fmt == "e4m3":
        byte = np.frexp(amax)[1] - 1 + 127 - 7
    else:
        mant, ex = np.frexp(amax / 6.0)
        byte = np.where(mant > 0.5, ex, ex - 1) + 127
    byte = np.clip(np.where(amax > 0, byte, 1), 1, 254)
    scaled = (w * np.exp2(127.0 - byte)[:, None, :]).reshape(k, n).astype(np.float32)
    by_word = np.ascontiguousarray(scaled.reshape(k // 512, 128, 4, n).transpose(0, 1, 3, 2))
    if fmt == "e4m3":
        words = by_word.astype(ml_dtypes.float8_e4m3fn).view(np.uint8)
    else:
        c = by_word.astype(ml_dtypes.float4_e2m1fn).view(np.uint8) & 0xF
        words = c[..., 0::2] | (c[..., 1::2] << 4)
    return np.ascontiguousarray(words), np.ascontiguousarray(byte.astype(np.uint8).reshape(k // 512, 16, n))


def unpack_weight(words, scales, fmt):
    g, p, n, _ = words.shape
    if fmt == "e4m3":
        vals = np.ascontiguousarray(words).view(ml_dtypes.float8_e4m3fn).astype(np.float64)
    else:
        nib = np.empty((g, p, n, 4), np.uint8)
        nib[..., 0::2] = words & 0xF
        nib[..., 1::2] = words >> 4
        vals = E2M1[nib]
    vals = vals * np.repeat(np.exp2(scales.astype(np.float64) - 127.0), 8, axis=1)[..., None]
    return vals.transpose(0, 1, 3, 2).reshape(g * 512, n)

def pack4(w):
    words, scales = pack_weight(w, "e2m1")
    return words.reshape(words.shape[0], 128, -1), scales


def unpack4(words, scales):
    return unpack_weight(words.reshape(words.shape[0], 128, -1, 2), scales, "e2m1")


def kspread(k):
    return np.exp2(np.repeat(np.random.randint(-6, 7, k // 32), 32).astype(np.float64))


DIM, H, HKV, D, B, S = 4096, 16, 4, 64, 2, 256
T = B * S


def rope_table():
    inv_freq = 1.0 / (10000.0 ** (np.arange(0, D, 2) / D))
    ang = np.arange(S)[:, None] * inv_freq[None, :]
    fc = np.stack([np.cos(ang), np.sin(ang)], axis=-1)
    return np.tile(fc, (B, 1, 1))


def rope(t, fc):
    t2 = t.reshape(t.shape[0], t.shape[1], D // 2, 2)
    cos = fc[:, None, :, 0]
    sin = fc[:, None, :, 1]
    r0 = t2[..., 0] * cos - t2[..., 1] * sin
    r1 = t2[..., 0] * sin + t2[..., 1] * cos
    return np.stack([r0, r1], axis=-1).reshape(t.shape)


def setup_inputs():
    s = kspread(DIM)
    x = np.random.standard_normal((T, DIM)) * s
    x_words, x_scales = pack4(x.T)
    freqs_cis = bf(rope_table())
    wq_words, wq_scales = pack4(np.random.standard_normal((DIM, H * D)) * 1.5 / np.sqrt(DIM) / s[:, None])
    wk_words, wk_scales = pack4(np.random.standard_normal((DIM, HKV * D)) * 1.5 / np.sqrt(DIM) / s[:, None])
    wv_words, wv_scales = pack4(np.random.standard_normal((DIM, HKV * D)) / np.sqrt(DIM) / s[:, None])
    return {"x_words": x_words, "x_scales": x_scales,
            "freqs_cis": freqs_cis,
            "wq_words": wq_words, "wq_scales": wq_scales,
            "wk_words": wk_words, "wk_scales": wk_scales,
            "wv_words": wv_words, "wv_scales": wv_scales}


def reference(x_words, x_scales, freqs_cis, wq_words, wq_scales, wk_words, wk_scales, wv_words, wv_scales):
    xq = unpack4(x_words, x_scales).T
    fc = f64(freqs_cis)
    q_rot = rope((xq @ unpack4(wq_words, wq_scales)).reshape(T, H, D), fc)
    k_rot = rope((xq @ unpack4(wk_words, wk_scales)).reshape(T, HKV, D), fc)
    v = (xq @ unpack4(wv_words, wv_scales)).reshape(T, HKV, D)
    return q_rot, k_rot, v

@@ -1,0 +1,201 @@
+from contextlib import ExitStack
+
+import concourse.mybir as mybir
+
+F32 = mybir.dt.float32
+BF16 = mybir.dt.bfloat16
+U8 = mybir.dt.uint8
+I32 = mybir.dt.int32
+FP4X4 = mybir.dt.float4_e2m1fn_x4
+MULT = mybir.AluOpType.mult
+ADD = mybir.AluOpType.add
+
+P = 128
+T = 512
+DIM = 4096
+PASSES = DIM // 512
+MT = T // P
+HD = 64
+NQ = 1024
+NKV = 256
+FLOPS = 2 * T * DIM * (NQ + 2 * NKV)
+
+BOTH = 2
+N_DUMMY = 8
+GPSIMD_ADDS = ("qa0", "qa1", "qa2", "qa3", "qb0", "qb1", "qb2", "qb3")
+
+
+def tile_attention_pa_kernel(
+    tc, x_words, x_scales, freqs_cis, wq_words, wq_scales, wk_words, wk_scales, wv_words, wv_scales, out_0, out_1, out_2
+):
+    nc = tc.nc
+    words_of = {"x": x_words, "q": wq_words, "k": wk_words, "v": wv_words}
+    scales_of = {"x": x_scales, "q": wq_scales, "k": wk_scales, "v": wv_scales}
+    with ExitStack() as ctx:
+        keep = ctx.enter_context(tc.tile_pool(name="keep", bufs=1))
+        psum = ctx.enter_context(tc.psum_pool(name="psum", bufs=1))
+        ctx.enter_context(tc.manual_schedule())
+
+        codes = {}
+        planes = {}
+
+        def load_codes(op, g0, g1, c0=0, c1=None):
+            words = words_of[op]
+            c1 = words.shape[2] // 2 if c1 is None else c1
+            t = keep.tile([P, g1 - g0, 2 * (c1 - c0)], U8, name="c_%s_%d_%d" % (op, g0, c0), align_bytes=64)
+            nc.sync.dma_start(
+                out=t[:].bitcast(I32),
+                in_=words[g0:g1, :, 2 * c0 : 2 * c1].rearrange("g p n -> p g n").bitcast(I32),
+            )
+            for g in range(g0, g1):
+                codes.setdefault((op, g), []).append((t, g - g0, c0, c1))
+
+        def make_planes(op, g0, g1, c0=0, c1=None):
+            c1 = scales_of[op].shape[2] if c1 is None else c1
+            t = keep.tile([P, g1 - g0, c1 - c0], U8, name="s_%s_%d_%d" % (op, g0, c0), align_bytes=64)
+            nc.vector.memset(t[:].bitcast(I32), 0)
+            for g in range(g0, g1):
+                planes.setdefault((op, g), []).append((t, g - g0, c0, c1))
+
+        def load_planes(op, g0, g1, c0=0, c1=None):
+            c1 = scales_of[op].shape[2] if c1 is None else c1
+            t = [e for e in planes[(op, g0)] if e[2] == c0][0][0]
+            for r in range(4):
+                nc.sync.dma_start(
+                    out=t[r : P : 32, :, :].bitcast(I32),
+                    in_=scales_of[op][g0:g1, r : 16 : 4, c0:c1].rearrange("g q n -> q g n").bitcast(I32),
+                )
+
+        def find(table, op, g, c0, n):
+            return [e for e in table[(op, g)] if e[2] <= c0 and c0 + n <= e[3]][0]
+
+        runs = [
+            ("x", 0, 2), ("q", 0, 2),
+            ("x", 2, 8), ("q", 2, 8, 0, 512),
+            ("q", 2, 8, 512, 1024),
+            ("k", 0, 8), ("v", 0, 8),
+        ]
+        for r in runs:
+            make_planes(*r)
+
+        zeros = keep.tile([P, 512], BF16, name="zeros")
+        nc.gpsimd.memset(zeros[:].bitcast(F32), 0.0)
+        fc = keep.tile([P, MT, HD], BF16, name="fc")
+        nc.gpsimd.dma_start(out=fc[:], in_=freqs_cis.rearrange("(m p) j t -> p m (j t)", p=P))
+        warm = keep.tile([P, 1], F32, name="warm")
+        nc.scalar.copy(out=warm[:], in_=zeros[:, 0:1])
+        dummy = psum.tile([P, 512], F32, name="dummy", tag="bank7")
+        for i in range(N_DUMMY):
+            nc.tensor.matmul(out=dummy[:], lhsT=zeros[:, 0:P], rhs=zeros[:], start=True, stop=True)
+
+        load_codes("x", 0, 1)
+        load_codes("q", 0, 1, 0, 512)
+        load_planes(*runs[0])
+        load_planes(*runs[1])
+        load_codes("q", 0, 1, 512, 1024)
+        load_codes("x", 1, 2)
+        load_codes("q", 1, 2)
+        load_planes(*runs[2])
+        load_planes(*runs[3])
+        load_codes("x", 2, 4)
+        load_codes("q", 2, 4, 0, 512)
+        load_codes("x", 4, 6)
+        load_codes("q", 4, 6, 0, 512)
+        load_codes("x", 6, 8)
+        load_codes("q", 6, 8, 0, 512)
+        load_planes(*runs[4])
+        load_codes("q", 2, 4, 512, 1024)
+        load_codes("q", 4, 6, 512, 1024)
+        load_codes("q", 6, 8, 512, 1024)
+        load_planes(*runs[5])
+        load_codes("k", 0, 4)
+        load_codes("k", 4, 8)
+        load_planes(*runs[6])
+        load_codes("v", 0, 4)
+        load_codes("v", 4, 8)
+
+        cc = keep.tile([P, MT, HD], F32, name="cc")
+        ss = keep.tile([P, MT, HD], F32, name="ss")
+        fcv = fc[:].rearrange("p m (j t) -> p (m j) t", t=2)
+        ccv = cc[:].rearrange("p m (j t) -> p (m j) t", t=2)
+        ssv = ss[:].rearrange("p m (j t) -> p (m j) t", t=2)
+        nc.vector.tensor_copy(out=ccv, in_=fcv[:, :, 0:1].to_broadcast([P, MT * HD // 2, 2]))
+        nc.vector.tensor_copy(out=ssv[:, :, 0:1], in_=fcv[:, :, 1:2])
+        nc.vector.tensor_scalar_mul(out=ssv[:, :, 1:2], in0=fcv[:, :, 1:2], scalar1=-1.0)
+
+        def mx_pass(acc, m, op, g, c0, n):
+            xt, xi, xc0, xc1 = find(codes, "x", g, P * m, P)
+            xp, xpi, xp0, xp1 = find(planes, "x", g, P * m, P)
+            wt, wi, wc0, wc1 = find(codes, op, g, c0, n)
+            wp, wpi, wp0, wp1 = find(planes, op, g, c0, n)
+            nc.tensor.matmul_mx(
+                out=acc[:],
+                lhsT=xt[:, xi, 2 * (P * m - xc0) : 2 * (P * (m + 1) - xc0)].bitcast(FP4X4),
+                lhsT_scale=xp[:, xpi, P * m - xp0 : P * (m + 1) - xp0],
+                rhs=wt[:, wi, 2 * (c0 - wc0) : 2 * (c0 + n - wc0)].bitcast(FP4X4),
+                rhs_scale=wp[:, wpi, c0 - wp0 : c0 + n - wp0],
+                start=(g == 0),
+                stop=(g == PASSES - 1),
+            )
+
+        def rope(acc, m, n, dst, label):
+            heads = n // HD
+            a = keep.tile([P, n], F32, name="a_" + label)
+            b = keep.tile([P, n], F32, name="b_" + label)
+            o = keep.tile([P, n], F32, name="o_" + label)
+            accv = acc[:].rearrange("p (h d) -> p h d", d=HD)
+            nc.vector.tensor_tensor(
+                out=a[:].rearrange("p (h d) -> p h d", d=HD), in0=accv,
+                in1=cc[:, m, :].unsqueeze(1).to_broadcast([P, heads, HD]), op=MULT,
+            )
+            nc.vector.tensor_tensor(
+                out=b[:].rearrange("p (h d) -> p h d", d=HD), in0=accv,
+                in1=ss[:, m, :].unsqueeze(1).to_broadcast([P, heads, HD]), op=MULT,
+            )
+            eng = nc.gpsimd if label in GPSIMD_ADDS else nc.vector
+            eng.tensor_tensor(
+                out=o[:].rearrange("p (j t) -> p j t", t=2),
+                in0=a[:].rearrange("p (j t) -> p j t", t=2),
+                in1=b[:].rearrange("p (j t) -> p j t", t=2)[:, :, ::-1],
+                op=ADD,
+            )
+            nc.sync.dma_start(out=dst, in_=o[:])
+
+        def q_dst(m, blk):
+            return out_0[P * m : P * (m + 1), 8 * blk : 8 * blk + 8, :].rearrange("p h d -> p (h d)")
+
+        acc_a = []
+        acc_b = []
+        for m in range(MT):
+            qa = psum.tile([P, 512], F32, name="qa%d" % m, tag="bank%d" % m)
+            acc_a.append(qa)
+        for m in range(MT):
+            qb = psum.tile([P, 512], F32, name="qb%d" % m, tag="bank%d" % (4 + m))
+            acc_b.append(qb)
+        for g in range(BOTH):
+            for m in range(MT):
+                mx_pass(acc_a[m], m, "q", g, 0, 512)
+            for m in range(MT):
+                mx_pass(acc_b[m], m, "q", g, 512, 512)
+        for g in range(BOTH, PASSES):
+            for m in range(MT):
+                mx_pass(acc_a[m], m, "q", g, 0, 512)
+                if g == PASSES - 1:
+                    rope(acc_a[m], m, 512, q_dst(m, 0), "qa%d" % m)
+        for m in range(MT):
+            for g in range(BOTH, PASSES):
+                mx_pass(acc_b[m], m, "q", g, 512, 512)
+            rope(acc_b[m], m, 512, q_dst(m, 1), "qb%d" % m)
+
+        for m in range(MT):
+            acc_k = psum.tile([P, NKV], F32, name="k%d" % m, tag="bank%d" % m)
+            for g in range(PASSES):
+                mx_pass(acc_k, m, "k", g, 0, NKV)
+            rope(acc_k, m, NKV, out_1[P * m : P * (m + 1), :, :].rearrange("p h d -> p (h d)"), "k%d" % m)
+        for m in range(MT):
+            acc_v = psum.tile([P, NKV], F32, name="v%d" % m, tag="bank%d" % (4 + m))
+            for g in range(PASSES):
+                mx_pass(acc_v, m, "v", g, 0, NKV)
+            vo = keep.tile([P, NKV], F32, name="vo%d" % m)
+            nc.scalar.copy(out=vo[:], in_=acc_v[:])
+            nc.scalar.dma_start(out=out_2[P * m : P * (m + 1), :, :].rearrange("p h d -> p (h d)"), in_=vo[:])

@@ -20,7 +20,7 @@ NQ = 1024
 NKV = 256
 FLOPS = 2 * T * DIM * (NQ + 2 * NKV)
 
-BOTH = 2
+BOTH = 3
 N_DUMMY = 8
 GPSIMD_ADDS = ("qa0", "qa1", "qa2", "qa3", "qb0", "qb1", "qb2", "qb3")
 
@@ -70,9 +70,9 @@ def tile_attention_pa_kernel(
             return [e for e in table[(op, g)] if e[2] <= c0 and c0 + n <= e[3]][0]
 
         runs = [
-            ("x", 0, 2), ("q", 0, 2),
-            ("x", 2, 8), ("q", 2, 8, 0, 512),
-            ("q", 2, 8, 512, 1024),
+            ("q", 0, 3), ("x", 0, 3),
+            ("x", 3, 8), ("q", 3, 8, 0, 512),
+            ("q", 3, 8, 512, 1024),
             ("k", 0, 8), ("v", 0, 8),
         ]
         for r in runs:
@@ -93,20 +93,20 @@ def tile_attention_pa_kernel(
         load_planes(*runs[0])
         load_planes(*runs[1])
         load_codes("q", 0, 1, 512, 1024)
-        load_codes("x", 1, 2)
+        load_codes("x", 1, 3)
         load_codes("q", 1, 2)
+        load_codes("q", 2, 3)
         load_planes(*runs[2])
         load_planes(*runs[3])
-        load_codes("x", 2, 4)
-        load_codes("q", 2, 4, 0, 512)
+        load_codes("x", 3, 4)
+        load_codes("q", 3, 4, 0, 512)
         load_codes("x", 4, 6)
         load_codes("q", 4, 6, 0, 512)
         load_codes("x", 6, 8)
         load_codes("q", 6, 8, 0, 512)
         load_planes(*runs[4])
-        load_codes("q", 2, 4, 512, 1024)
-        load_codes("q", 4, 6, 512, 1024)
-        load_codes("q", 6, 8, 512, 1024)
+        load_codes("q", 3, 5, 512, 1024)
+        load_codes("q", 5, 8, 512, 1024)
         load_planes(*runs[5])
         load_codes("k", 0, 4)
         load_codes("k", 4, 8)

@@ -51,7 +51,7 @@ def tile_attention_pa_kernel(
                 codes.setdefault((op, g), []).append((t, g - g0, c0, c1))
 
         def make_planes(op, g0, g1, c0=0, c1=None):
-            c1 = scales_of[op].shape[2] if c1 is None else c1
+            c1 = (2 * NKV if op == "kv" else scales_of[op].shape[2]) if c1 is None else c1
             t = keep.tile([P, g1 - g0, c1 - c0], U8, name="s_%s_%d_%d" % (op, g0, c0), align_bytes=64)
             nc.vector.memset(t[:].bitcast(I32), 0)
             for g in range(g0, g1):
@@ -66,6 +66,26 @@ def tile_attention_pa_kernel(
                     in_=scales_of[op][g0:g1, r : 16 : 4, c0:c1].rearrange("g q n -> q g n").bitcast(I32),
                 )
 
+        def make_kv_codes(g0, g1):
+            t = keep.tile([P, g1 - g0, 4 * NKV], U8, name="c_kv_%d" % g0, align_bytes=64)
+            for g in range(g0, g1):
+                codes.setdefault(("kv", g), []).append((t, g - g0, 0, 2 * NKV))
+            return t
+
+        def load_kv_codes(t, half, words, g0, g1):
+            nc.sync.dma_start(
+                out=t[:, :, 2 * NKV * half : 2 * NKV * (half + 1)].bitcast(I32),
+                in_=words[g0:g1].rearrange("g p n -> p g n").bitcast(I32),
+            )
+
+        def load_kv_planes(half, scales):
+            t = planes[("kv", 0)][0][0]
+            for r in range(4):
+                nc.sync.dma_start(
+                    out=t[r : P : 32, :, NKV * half : NKV * (half + 1)].bitcast(I32),
+                    in_=scales[:, r : 16 : 4, :].rearrange("g q n -> q g n").bitcast(I32),
+                )
+
         def find(table, op, g, c0, n):
             return [e for e in table[(op, g)] if e[2] <= c0 and c0 + n <= e[3]][0]
 
@@ -73,7 +93,7 @@ def tile_attention_pa_kernel(
             ("q", 0, 3), ("x", 0, 3),
             ("x", 3, 8), ("q", 3, 8, 0, 512),
             ("q", 3, 8, 512, 1024),
-            ("k", 0, 8), ("v", 0, 8),
+            ("kv", 0, 8),
         ]
         for r in runs:
             make_planes(*r)
@@ -107,12 +127,12 @@ def tile_attention_pa_kernel(
         load_planes(*runs[4])
         load_codes("q", 3, 5, 512, 1024)
         load_codes("q", 5, 8, 512, 1024)
-        load_planes(*runs[5])
-        load_codes("k", 0, 4)
-        load_codes("k", 4, 8)
-        load_planes(*runs[6])
-        load_codes("v", 0, 4)
-        load_codes("v", 4, 8)
+        load_kv_planes(0, wk_scales)
+        load_kv_planes(1, wv_scales)
+        for g0 in (0, 4):
+            kv = make_kv_codes(g0, g0 + 4)
+            load_kv_codes(kv, 0, wk_words, g0, g0 + 4)
+            load_kv_codes(kv, 1, wv_words, g0, g0 + 4)
 
         cc = keep.tile([P, MT, HD], F32, name="cc")
         ss = keep.tile([P, MT, HD], F32, name="ss")
@@ -187,15 +207,26 @@ def tile_attention_pa_kernel(
                 mx_pass(acc_b[m], m, "q", g, 512, 512)
             rope(acc_b[m], m, 512, q_dst(m, 1), "qb%d" % m)
 
-        for m in range(MT):
-            acc_k = psum.tile([P, NKV], F32, name="k%d" % m, tag="bank%d" % m)
-            for g in range(PASSES):
-                mx_pass(acc_k, m, "k", g, 0, NKV)
-            rope(acc_k, m, NKV, out_1[P * m : P * (m + 1), :, :].rearrange("p h d -> p (h d)"), "k%d" % m)
-        for m in range(MT):
-            acc_v = psum.tile([P, NKV], F32, name="v%d" % m, tag="bank%d" % (4 + m))
-            for g in range(PASSES):
-                mx_pass(acc_v, m, "v", g, 0, NKV)
+        def k_dst(m):
+            return out_1[P * m : P * (m + 1), :, :].rearrange("p h d -> p (h d)")
+
+        def v_out(acc, m):
             vo = keep.tile([P, NKV], F32, name="vo%d" % m)
-            nc.scalar.copy(out=vo[:], in_=acc_v[:])
+            nc.scalar.copy(out=vo[:], in_=acc)
             nc.scalar.dma_start(out=out_2[P * m : P * (m + 1), :, :].rearrange("p h d -> p (h d)"), in_=vo[:])
+
+        for m in range(MT - 1):
+            acc_kv = psum.tile([P, 2 * NKV], F32, name="kv%d" % m, tag="bank%d" % m)
+            for g in range(PASSES):
+                mx_pass(acc_kv, m, "kv", g, 0, 2 * NKV)
+            rope(acc_kv[:, 0:NKV], m, NKV, k_dst(m), "k%d" % m)
+            v_out(acc_kv[:, NKV : 2 * NKV], m)
+        m = MT - 1
+        acc_k = psum.tile([P, NKV], F32, name="k%d" % m, tag="bank3")
+        for g in range(PASSES):
+            mx_pass(acc_k, m, "kv", g, 0, NKV)
+        rope(acc_k, m, NKV, k_dst(m), "k%d" % m)
+        acc_v = psum.tile([P, NKV], F32, name="v%d" % m, tag="bank4")
+        for g in range(PASSES):
+            mx_pass(acc_v, m, "kv", g, NKV, NKV)
+        v_out(acc_v[:], m)

@@ -22,6 +22,7 @@ FLOPS = 2 * T * DIM * (NQ + 2 * NKV)
 
 BOTH = 3
 N_DUMMY = 8
+PHASE = {"wc": 0, "ws": 64, "xc": 128, "xs": 192}
 GPSIMD_ADDS = ("qa0", "qa1", "qa2", "qa3", "qb0", "qb1", "qb2", "qb3")
 
 
@@ -39,12 +40,17 @@ def tile_attention_pa_kernel(
         codes = {}
         planes = {}
 
+        def phased(kind, n, width, name):
+            ph = PHASE[kind]
+            whole = keep.tile([P, ph + n * width], U8, name=name, align_bytes=256)
+            return whole, whole[:, ph : ph + n * width].rearrange("p (g n) -> p g n", g=n)
+
         def load_codes(op, g0, g1, c0=0, c1=None):
             words = words_of[op]
             c1 = words.shape[2] // 2 if c1 is None else c1
-            t = keep.tile([P, g1 - g0, 2 * (c1 - c0)], U8, name="c_%s_%d_%d" % (op, g0, c0), align_bytes=64)
+            whole, t = phased("xc" if op == "x" else "wc", g1 - g0, 2 * (c1 - c0), "c_%s_%d_%d" % (op, g0, c0))
             nc.sync.dma_start(
-                out=t[:].bitcast(I32),
+                out=t.bitcast(I32),
                 in_=words[g0:g1, :, 2 * c0 : 2 * c1].rearrange("g p n -> p g n").bitcast(I32),
             )
             for g in range(g0, g1):
@@ -52,8 +58,8 @@ def tile_attention_pa_kernel(
 
         def make_planes(op, g0, g1, c0=0, c1=None):
             c1 = (2 * NKV if op == "kv" else scales_of[op].shape[2]) if c1 is None else c1
-            t = keep.tile([P, g1 - g0, c1 - c0], U8, name="s_%s_%d_%d" % (op, g0, c0), align_bytes=64)
-            nc.vector.memset(t[:].bitcast(I32), 0)
+            whole, t = phased("xs" if op == "x" else "ws", g1 - g0, c1 - c0, "s_%s_%d_%d" % (op, g0, c0))
+            nc.vector.memset(whole[:].bitcast(I32), 0)
             for g in range(g0, g1):
                 planes.setdefault((op, g), []).append((t, g - g0, c0, c1))
 
@@ -67,7 +73,7 @@ def tile_attention_pa_kernel(
                 )
 
         def make_kv_codes(g0, g1):
-            t = keep.tile([P, g1 - g0, 4 * NKV], U8, name="c_kv_%d" % g0, align_bytes=64)
+            whole, t = phased("wc", g1 - g0, 4 * NKV, "c_kv_%d" % g0)
             for g in range(g0, g1):
                 codes.setdefault(("kv", g), []).append((t, g - g0, 0, 2 * NKV))
             return t

@@ -107,7 +107,6 @@ def tile_attention_pa_kernel(
         zeros = keep.tile([P, 512], BF16, name="zeros")
         nc.gpsimd.memset(zeros[:].bitcast(F32), 0.0)
         fc = keep.tile([P, MT, HD], BF16, name="fc")
-        nc.gpsimd.dma_start(out=fc[:], in_=freqs_cis.rearrange("(m p) j t -> p m (j t)", p=P))
         warm = keep.tile([P, 1], F32, name="warm")
         nc.scalar.copy(out=warm[:], in_=zeros[:, 0:1])
         dummy = psum.tile([P, 512], F32, name="dummy", tag="bank7")
@@ -122,6 +121,7 @@ def tile_attention_pa_kernel(
         load_codes("x", 1, 3)
         load_codes("q", 1, 2)
         load_codes("q", 2, 3)
+        nc.sync.dma_start(out=fc[:], in_=freqs_cis.rearrange("(m p) j t -> p m (j t)", p=P))
         load_planes(*runs[2])
         load_planes(*runs[3])
         load_codes("x", 3, 4)

from contextlib import ExitStack

import concourse.mybir as mybir

F32 = mybir.dt.float32
BF16 = mybir.dt.bfloat16
U8 = mybir.dt.uint8
I32 = mybir.dt.int32
FP4X4 = mybir.dt.float4_e2m1fn_x4
MULT = mybir.AluOpType.mult
ADD = mybir.AluOpType.add

P = 128
T = 512
DIM = 4096
PASSES = DIM // 512
MT = T // P
HD = 64
NQ = 1024
NKV = 256
FLOPS = 2 * T * DIM * (NQ + 2 * NKV)

BOTH = 3
N_DUMMY = 8
PHASE = {"wc": 0, "ws": 64, "xc": 128, "xs": 192}
GPSIMD_ADDS = ("qa0", "qa1", "qa2", "qa3", "qb0", "qb1", "qb2", "qb3")


def tile_attention_pa_kernel(
    tc, x_words, x_scales, freqs_cis, wq_words, wq_scales, wk_words, wk_scales, wv_words, wv_scales, out_0, out_1, out_2
):
    nc = tc.nc
    words_of = {"x": x_words, "q": wq_words, "k": wk_words, "v": wv_words}
    scales_of = {"x": x_scales, "q": wq_scales, "k": wk_scales, "v": wv_scales}
    with ExitStack() as ctx:
        keep = ctx.enter_context(tc.tile_pool(name="keep", bufs=1))
        psum = ctx.enter_context(tc.psum_pool(name="psum", bufs=1))
        ctx.enter_context(tc.manual_schedule())

        codes = {}
        planes = {}

        def phased(kind, n, width, name):
            ph = PHASE[kind]
            whole = keep.tile([P, ph + n * width], U8, name=name, align_bytes=256)
            return whole, whole[:, ph : ph + n * width].rearrange("p (g n) -> p g n", g=n)

        def load_codes(op, g0, g1, c0=0, c1=None):
            words = words_of[op]
            c1 = words.shape[2] // 2 if c1 is None else c1
            whole, t = phased("xc" if op == "x" else "wc", g1 - g0, 2 * (c1 - c0), "c_%s_%d_%d" % (op, g0, c0))
            nc.sync.dma_start(
                out=t.bitcast(I32),
                in_=words[g0:g1, :, 2 * c0 : 2 * c1].rearrange("g p n -> p g n").bitcast(I32),
            )
            for g in range(g0, g1):
                codes.setdefault((op, g), []).append((t, g - g0, c0, c1))

        def make_planes(op, g0, g1, c0=0, c1=None):
            c1 = (2 * NKV if op == "kv" else scales_of[op].shape[2]) if c1 is None else c1
            whole, t = phased("xs" if op == "x" else "ws", g1 - g0, c1 - c0, "s_%s_%d_%d" % (op, g0, c0))
            nc.vector.memset(whole[:].bitcast(I32), 0)
            for g in range(g0, g1):
                planes.setdefault((op, g), []).append((t, g - g0, c0, c1))

        def load_planes(op, g0, g1, c0=0, c1=None):
            c1 = scales_of[op].shape[2] if c1 is None else c1
            t = [e for e in planes[(op, g0)] if e[2] == c0][0][0]
            for r in range(4):
                nc.sync.dma_start(
                    out=t[r : P : 32, :, :].bitcast(I32),
                    in_=scales_of[op][g0:g1, r : 16 : 4, c0:c1].rearrange("g q n -> q g n").bitcast(I32),
                )

        def make_kv_codes(g0, g1):
            whole, t = phased("wc", g1 - g0, 4 * NKV, "c_kv_%d" % g0)
            for g in range(g0, g1):
                codes.setdefault(("kv", g), []).append((t, g - g0, 0, 2 * NKV))
            return t

        def load_kv_codes(t, half, words, g0, g1):
            nc.sync.dma_start(
                out=t[:, :, 2 * NKV * half : 2 * NKV * (half + 1)].bitcast(I32),
                in_=words[g0:g1].rearrange("g p n -> p g n").bitcast(I32),
            )

        def load_kv_planes(half, scales):
            t = planes[("kv", 0)][0][0]
            for r in range(4):
                nc.sync.dma_start(
                    out=t[r : P : 32, :, NKV * half : NKV * (half + 1)].bitcast(I32),
                    in_=scales[:, r : 16 : 4, :].rearrange("g q n -> q g n").bitcast(I32),
                )

        def find(table, op, g, c0, n):
            return [e for e in table[(op, g)] if e[2] <= c0 and c0 + n <= e[3]][0]

        runs = [
            ("q", 0, 3), ("x", 0, 3),
            ("x", 3, 8), ("q", 3, 8, 0, 512),
            ("q", 3, 8, 512, 1024),
            ("kv", 0, 8),
        ]
        for r in runs:
            make_planes(*r)

        zeros = keep.tile([P, 512], BF16, name="zeros")
        nc.gpsimd.memset(zeros[:].bitcast(F32), 0.0)
        fc = keep.tile([P, MT, HD], BF16, name="fc")
        warm = keep.tile([P, 1], F32, name="warm")
        nc.scalar.copy(out=warm[:], in_=zeros[:, 0:1])
        dummy = psum.tile([P, 512], F32, name="dummy", tag="bank7")
        for i in range(N_DUMMY):
            nc.tensor.matmul(out=dummy[:], lhsT=zeros[:, 0:P], rhs=zeros[:], start=True, stop=True)

        load_codes("x", 0, 1)
        load_codes("q", 0, 1, 0, 512)
        load_planes(*runs[0])
        load_planes(*runs[1])
        load_codes("q", 0, 1, 512, 1024)
        load_codes("x", 1, 3)
        load_codes("q", 1, 2)
        load_codes("q", 2, 3)
        nc.sync.dma_start(out=fc[:], in_=freqs_cis.rearrange("(m p) j t -> p m (j t)", p=P))
        load_planes(*runs[2])
        load_planes(*runs[3])
        load_codes("x", 3, 4)
        load_codes("q", 3, 4, 0, 512)
        load_codes("x", 4, 6)
        load_codes("q", 4, 6, 0, 512)
        load_codes("x", 6, 8)
        load_codes("q", 6, 8, 0, 512)
        load_planes(*runs[4])
        load_codes("q", 3, 5, 512, 1024)
        load_codes("q", 5, 8, 512, 1024)
        load_kv_planes(0, wk_scales)
        load_kv_planes(1, wv_scales)
        for g0 in (0, 4):
            kv = make_kv_codes(g0, g0 + 4)
            load_kv_codes(kv, 0, wk_words, g0, g0 + 4)
            load_kv_codes(kv, 1, wv_words, g0, g0 + 4)

        cc = keep.tile([P, MT, HD], F32, name="cc")
        ss = keep.tile([P, MT, HD], F32, name="ss")
        fcv = fc[:].rearrange("p m (j t) -> p (m j) t", t=2)
        ccv = cc[:].rearrange("p m (j t) -> p (m j) t", t=2)
        ssv = ss[:].rearrange("p m (j t) -> p (m j) t", t=2)
        nc.vector.tensor_copy(out=ccv, in_=fcv[:, :, 0:1].to_broadcast([P, MT * HD // 2, 2]))
        nc.vector.tensor_copy(out=ssv[:, :, 0:1], in_=fcv[:, :, 1:2])
        nc.vector.tensor_scalar_mul(out=ssv[:, :, 1:2], in0=fcv[:, :, 1:2], scalar1=-1.0)

        def mx_pass(acc, m, op, g, c0, n):
            xt, xi, xc0, xc1 = find(codes, "x", g, P * m, P)
            xp, xpi, xp0, xp1 = find(planes, "x", g, P * m, P)
            wt, wi, wc0, wc1 = find(codes, op, g, c0, n)
            wp, wpi, wp0, wp1 = find(planes, op, g, c0, n)
            nc.tensor.matmul_mx(
                out=acc[:],
                lhsT=xt[:, xi, 2 * (P * m - xc0) : 2 * (P * (m + 1) - xc0)].bitcast(FP4X4),
                lhsT_scale=xp[:, xpi, P * m - xp0 : P * (m + 1) - xp0],
                rhs=wt[:, wi, 2 * (c0 - wc0) : 2 * (c0 + n - wc0)].bitcast(FP4X4),
                rhs_scale=wp[:, wpi, c0 - wp0 : c0 + n - wp0],
                start=(g == 0),
                stop=(g == PASSES - 1),
            )

        def rope(acc, m, n, dst, label):
            heads = n // HD
            a = keep.tile([P, n], F32, name="a_" + label)
            b = keep.tile([P, n], F32, name="b_" + label)
            o = keep.tile([P, n], F32, name="o_" + label)
            accv = acc[:].rearrange("p (h d) -> p h d", d=HD)
            nc.vector.tensor_tensor(
                out=a[:].rearrange("p (h d) -> p h d", d=HD), in0=accv,
                in1=cc[:, m, :].unsqueeze(1).to_broadcast([P, heads, HD]), op=MULT,
            )
            nc.vector.tensor_tensor(
                out=b[:].rearrange("p (h d) -> p h d", d=HD), in0=accv,
                in1=ss[:, m, :].unsqueeze(1).to_broadcast([P, heads, HD]), op=MULT,
            )
            eng = nc.gpsimd if label in GPSIMD_ADDS else nc.vector
            eng.tensor_tensor(
                out=o[:].rearrange("p (j t) -> p j t", t=2),
                in0=a[:].rearrange("p (j t) -> p j t", t=2),
                in1=b[:].rearrange("p (j t) -> p j t", t=2)[:, :, ::-1],
                op=ADD,
            )
            nc.sync.dma_start(out=dst, in_=o[:])

        def q_dst(m, blk):
            return out_0[P * m : P * (m + 1), 8 * blk : 8 * blk + 8, :].rearrange("p h d -> p (h d)")

        acc_a = []
        acc_b = []
        for m in range(MT):
            qa = psum.tile([P, 512], F32, name="qa%d" % m, tag="bank%d" % m)
            acc_a.append(qa)
        for m in range(MT):
            qb = psum.tile([P, 512], F32, name="qb%d" % m, tag="bank%d" % (4 + m))
            acc_b.append(qb)
        for g in range(BOTH):
            for m in range(MT):
                mx_pass(acc_a[m], m, "q", g, 0, 512)
            for m in range(MT):
                mx_pass(acc_b[m], m, "q", g, 512, 512)
        for g in range(BOTH, PASSES):
            for m in range(MT):
                mx_pass(acc_a[m], m, "q", g, 0, 512)
                if g == PASSES - 1:
                    rope(acc_a[m], m, 512, q_dst(m, 0), "qa%d" % m)
        for m in range(MT):
            for g in range(BOTH, PASSES):
                mx_pass(acc_b[m], m, "q", g, 512, 512)
            rope(acc_b[m], m, 512, q_dst(m, 1), "qb%d" % m)

        def k_dst(m):
            return out_1[P * m : P * (m + 1), :, :].rearrange("p h d -> p (h d)")

        def v_out(acc, m):
            vo = keep.tile([P, NKV], F32, name="vo%d" % m)
            nc.scalar.copy(out=vo[:], in_=acc)
            nc.scalar.dma_start(out=out_2[P * m : P * (m + 1), :, :].rearrange("p h d -> p (h d)"), in_=vo[:])

        for m in range(MT - 1):
            acc_kv = psum.tile([P, 2 * NKV], F32, name="kv%d" % m, tag="bank%d" % m)
            for g in range(PASSES):
                mx_pass(acc_kv, m, "kv", g, 0, 2 * NKV)
            rope(acc_kv[:, 0:NKV], m, NKV, k_dst(m), "k%d" % m)
            v_out(acc_kv[:, NKV : 2 * NKV], m)
        m = MT - 1
        acc_k = psum.tile([P, NKV], F32, name="k%d" % m, tag="bank3")
        for g in range(PASSES):
            mx_pass(acc_k, m, "kv", g, 0, NKV)
        rope(acc_k, m, NKV, k_dst(m), "k%d" % m)
        acc_v = psum.tile([P, NKV], F32, name="v%d" % m, tag="bank4")
        for g in range(PASSES):
            mx_pass(acc_v, m, "kv", g, NKV, NKV)
        v_out(acc_v[:], m)
